import numpy as np
import ml_dtypes


def mxq(x, axis, fmt="e4m3"):
    dtype, down = {"e4m3": (ml_dtypes.float8_e4m3fn, 7), "e5m2": (ml_dtypes.float8_e5m2, 14)}[fmt]
    v = np.moveaxis(np.asarray(x, np.float32).astype(ml_dtypes.bfloat16).astype(np.float64), axis, -1)
    blocks = v.reshape(v.shape[:-1] + (-1, 32))
    amax = np.abs(blocks).max(-1, keepdims=True)
    byte = np.maximum(np.where(amax > 0, np.frexp(amax)[1] - 1 + 127, 0) - down, 1)
    scale = np.exp2(byte - 127.0)
    codes = (blocks / scale).astype(np.float32).astype(dtype).astype(np.float64)
    return np.moveaxis((codes * scale).reshape(v.shape), -1, axis)


WIDE = False


def mx_kscale(k):
    if not WIDE:
        return np.ones(k)
    levels = np.array([10, -10, 5, -5, 0])
    if k % 512:
        return np.exp2(np.random.permutation(np.resize(levels, k // 32))).repeat(32)
    a = np.empty((k // 512, 16))
    for p in range(k // 512):
        a[p, :8] = np.random.permutation(np.resize(levels, 8))
        for g in range(8):
            far = levels[np.abs(levels - a[p, g]) >= 10]
            a[p, g + 8] = far[np.random.randint(len(far))]
    return np.exp2(a.ravel()).repeat(32)


BF16 = ml_dtypes.bfloat16


def bf(x):
    return np.asarray(x, np.float32).astype(BF16)


def f64(x):
    return np.asarray(x).astype(np.float64)


B, C, H, D, N, CO = 16, 128, 2048, 512, 4, 128
NC = N * C
EPS = 1e-5


def bn(v, gamma, beta, axes):
    mean = v.mean(axis=axes, keepdims=True)
    var = v.var(axis=axes, keepdims=True)
    return (v - mean) / np.sqrt(var + EPS) * gamma + beta


def setup_inputs():
    u = mx_kscale(NC)
    head = np.maximum(np.random.standard_normal((N, B, C, D)), 0.0) + 0.25 * np.random.standard_normal((N, B, C, D))
    return {'head_res': bf(head * u.reshape(N, 1, C, 1)),
            'W_merge': bf(np.random.standard_normal((CO, NC)) / np.sqrt(NC) / u[None, :]),
            'g_m': bf(1.0 + 0.1 * np.random.standard_normal(CO)),
            'b_m': bf(0.1 * np.random.standard_normal(CO))}


def reference(head_res, W_merge, g_m, b_m):
    cat = f64(head_res).transpose(1, 0, 2, 3).reshape(B, NC, D)
    m = mxq(f64(W_merge), 1, 'e4m3')[None] @ mxq(cat, 1, 'e4m3')
    m = bn(m, f64(g_m)[None, :, None], f64(b_m)[None, :, None], (0, 2))
    return np.maximum(m, 0.0)

@@ -1,0 +1,233 @@
+from contextlib import ExitStack
+
+import concourse.mybir as mybir
+from concourse.masks import make_identity
+
+FLOPS = 2 * 16 * 128 * 512 * 512
+
+F32 = mybir.dt.float32
+BF16 = mybir.dt.bfloat16
+U32 = mybir.dt.uint32
+U8 = mybir.dt.uint8
+FP8X4 = mybir.dt.float8_e4m3fn_x4
+ALU = mybir.AluOpType
+ACT = mybir.ActivationFunctionType
+AX = mybir.AxisListType
+
+P = 128
+NH = 4
+NB = 16
+D = 512
+EPS = 1e-5
+CHUNKS = [1] * 16
+CV = 336
+CV_LAST = 384
+MBUFS = 7
+HALF = 256
+PIV = 64
+MANUAL = True
+LAG_SWITCH = 99
+
+
+def tile_block_height_reducing_filtering_pb_t_kernel(tc, head_res, W_merge, g_m, b_m, out):
+    nc = tc.nc
+    with ExitStack() as ctx:
+        consts = ctx.enter_context(tc.tile_pool(name="consts", bufs=1))
+        rawp = ctx.enter_context(tc.tile_pool(name="rawp", bufs=1))
+        grpp = ctx.enter_context(tc.tile_pool(name="grpp", bufs=4))
+        codep = ctx.enter_context(tc.tile_pool(name="codep", bufs=1))
+        outp = ctx.enter_context(tc.tile_pool(name="outp", bufs=1))
+        small = ctx.enter_context(tc.tile_pool(name="small", bufs=1))
+        psum = ctx.enter_context(tc.psum_pool(name="psum", bufs=MBUFS))
+        if MANUAL:
+            ctx.enter_context(tc.manual_schedule())
+
+        w_sb = consts.tile([P, NH * P], BF16, name="w_sb")
+        nc.scalar.dma_start(out=w_sb[:], in_=W_merge)
+        g_bf = small.tile([P, 1], BF16, name="g_bf")
+        b_bf = small.tile([P, 1], BF16, name="b_bf")
+
+        raw_of = []
+        b0 = 0
+        for ci, nb in enumerate(CHUNKS):
+            raw = rawp.tile([P, nb, NH * D], BF16, name="raw%d" % ci)
+            for j in range(nb):
+                for n in (0, 2, 1, 3):
+                    nc.sync.dma_start(
+                        out=raw[32 * n : 32 * n + 32, j, :],
+                        in_=head_res[n, b0 + j].rearrange("(q t) d -> q (t d)", t=4),
+                    )
+            for j in range(nb):
+                raw_of.append((raw, j))
+            b0 += nb
+
+        one = small.tile([P, 1], F32, name="one")
+        nc.vector.memset(one[:], 1.0)
+        warm = small.tile([P, 1], F32, name="warm")
+        nc.scalar.activation(out=warm[:], in_=one[:], func=ACT.Abs_reciprocal_sqrt)
+        ident = consts.tile([P, P], BF16, name="ident")
+        make_identity(nc, ident[:])
+
+        w_perm = consts.tile([P, 4, P], BF16, name="w_perm")
+        nc.vector.tensor_copy(out=w_perm[:], in_=w_sb[:].rearrange("o (p t) -> o t p", t=4))
+        wT_ps = psum.tile([P, 4, P], BF16, name="wT_ps", tag="m")
+        for t in range(4):
+            nc.tensor.transpose(wT_ps[:, t, :], w_perm[:, t, :], ident[:])
+        w_grp = consts.tile([P, P, 4], BF16, name="w_grp", align_bytes=64)
+        w_codes = consts.tile([P, P], U32, name="w_codes", align_bytes=64)
+        w_scales = consts.tile([P, P], U8, name="w_scales", align_bytes=64)
+
+        g32 = small.tile([P, 1], F32, name="g32")
+        b32 = small.tile([P, 1], F32, name="b32")
+
+        acc = psum.tile([P, D], F32, name="acc", tag="acc", bufs=1)
+        ss = small.tile([P, NB], F32, name="ss")
+        junk = consts.tile([P, D], F32, name="junk")
+        negc = small.tile([P, 1], F32, name="negc")
+
+        grp_of = {}
+        codes_of = {}
+        scales_of = {}
+        m_of = {}
+
+        def regroup_part(b, d0, d1):
+            raw, j = raw_of[b]
+            grp = grp_of[b]
+            src = raw[:, j, :].rearrange("p (t d) -> p t d", t=4)
+            dv = d0 + (d1 - d0) * (CV if b < NB - 3 else CV_LAST) // D
+            nc.vector.tensor_copy(
+                out=grp[:, d0:dv, :].rearrange("p (c i) t -> p c t i", i=4),
+                in_=src[:, :, d0:dv].rearrange("p t (c i) -> p c t i", i=4),
+            )
+            nc.scalar.copy(
+                out=grp[:, dv:d1, :].rearrange("p (c i) t -> p c t i", i=4),
+                in_=src[:, :, dv:d1].rearrange("p t (c i) -> p c t i", i=4),
+            )
+
+        def regroup(b):
+            grp = grpp.tile([P, D, 4], BF16, name="grp", align_bytes=64)
+            grp_of[b] = grp
+            regroup_part(b, 0, D)
+
+        def quantise(b):
+            codes = codep.tile([P, D], U32, name="codes%d" % b, align_bytes=64)
+            scales = codep.tile([P, D], U8, name="scales%d" % b, align_bytes=64)
+            codes_of[b] = codes
+            scales_of[b] = scales
+            nc.vector.quantize_mx(
+                out=codes[:].bitcast(FP8X4),
+                scales=scales[:],
+                in_=grp_of[b][:].rearrange("p d t -> p (d t)"),
+            )
+
+        def product(dst, b, start, stop):
+            nc.tensor.matmul_mx(
+                out=dst,
+                lhsT=w_codes[:].bitcast(FP8X4),
+                lhsT_scale=w_scales[:],
+                rhs=codes_of[b][:].bitcast(FP8X4),
+                rhs_scale=scales_of[b][:],
+                start=start,
+                stop=stop,
+            )
+
+        def multiply(b):
+            product(acc[:], b, b == 0, b == NB - 1)
+            m = psum.tile([P, D], F32, name="m%d" % b, tag="m")
+            m_of[b] = m
+            product(m[:], b, True, True)
+
+        def squares(b):
+            nc.scalar.activation(
+                out=junk[:], in_=m_of[b][:], func=ACT.Square, bias=negc[:, 0:1], scale=1.0,
+                accum_out=ss[:, b : b + 1],
+            )
+
+        sq_next = 0
+        for s in range(NB + 1):
+            if s < NB:
+                regroup(s)
+            if s == 0:
+                nc.scalar.copy(out=w_grp[:], in_=wT_ps[:].rearrange("p t o -> p o t"))
+            if s == 1:
+                nc.vector.quantize_mx(
+                    out=w_codes[:].bitcast(FP8X4), scales=w_scales[:],
+                    in_=w_grp[:].rearrange("p o t -> p (o t)"),
+                )
+            if s >= 1:
+                quantise(s - 1)
+                multiply(s - 1)
+            if s == 2:
+                nc.scalar.activation(
+                    out=junk[:, 0:PIV], in_=m_of[0][:, 0:PIV], func=ACT.Identity, scale=-1.0 / PIV, accum_out=negc[:]
+                )
+            if s == 12:
+                with nc.allow_non_contiguous_dma(reason="one gain and one shift per partition, 128 elements each"):
+                    nc.scalar.dma_start(out=g_bf[:], in_=g_m.rearrange("(o u) -> o u", u=1))
+                    nc.scalar.dma_start(out=b_bf[:], in_=b_m.rearrange("(o u) -> o u", u=1))
+            lag = 3 if s < LAG_SWITCH else 2
+            while sq_next <= s - lag:
+                squares(sq_next)
+                sq_next += 1
+        inv = 1.0 / (NB * D)
+        ssp = small.tile([P, 1], F32, name="ssp")
+        bias2 = small.tile([P, 1], F32, name="bias2")
+        bias2b = small.tile([P, 1], F32, name="bias2b")
+        s1 = small.tile([P, 1], F32, name="s1")
+        dpos = small.tile([P, 1], F32, name="dpos")
+        dneg = small.tile([P, 1], F32, name="dneg")
+        nmean = small.tile([P, 1], F32, name="nmean")
+        ngm = small.tile([P, 1], F32, name="ngm")
+        bias3 = small.tile([P, 1], F32, name="bias3")
+        rstd = small.tile([P, 1], F32, name="rstd")
+        gain = small.tile([P, 1], F32, name="gain")
+        shift = small.tile([P, 1], F32, name="shift")
+        nc.vector.tensor_copy(out=g32[:], in_=g_bf[:])
+        nc.vector.tensor_copy(out=b32[:], in_=b_bf[:])
+        nc.vector.reduce_sum(out=ssp[:], in_=ss[:, 0 : NB - 2], axis=AX.X)
+        nc.vector.tensor_scalar(out=bias2[:], in0=ssp[:], scalar1=inv, scalar2=EPS, op0=ALU.mult, op1=ALU.add)
+        while sq_next < NB:
+            squares(sq_next)
+            sq_next += 1
+        nc.vector.reduce_sum(out=s1[:], in_=acc[:], axis=AX.X)
+        nc.vector.tensor_scalar(out=dpos[:], in0=s1[:], scalar1=inv, scalar2=negc[:, 0:1], op0=ALU.mult, op1=ALU.add)
+        nc.vector.tensor_scalar(
+            out=dneg[:], in0=s1[:], scalar1=-inv, scalar2=negc[:, 0:1], op0=ALU.mult, op1=ALU.subtract
+        )
+        nc.vector.scalar_tensor_tensor(
+            out=bias2b[:], in0=ss[:, NB - 2 : NB - 1], scalar=inv, in1=bias2[:], op0=ALU.mult, op1=ALU.add
+        )
+        nc.vector.scalar_tensor_tensor(
+            out=bias3[:], in0=dpos[:], scalar=dneg[:, 0:1], in1=bias2b[:], op0=ALU.mult, op1=ALU.add
+        )
+        nc.scalar.activation(
+            out=rstd[:], in_=ss[:, NB - 1 : NB], func=ACT.Abs_reciprocal_sqrt, bias=bias3[:, 0:1], scale=inv
+        )
+        nc.vector.tensor_scalar(out=nmean[:], in0=s1[:], scalar1=-inv, scalar2=None, op0=ALU.mult)
+        nc.vector.tensor_tensor(out=ngm[:], in0=nmean[:], in1=g32[:], op=ALU.mult)
+        nc.vector.tensor_tensor(out=gain[:], in0=g32[:], in1=rstd[:], op=ALU.mult)
+        nc.vector.scalar_tensor_tensor(
+            out=shift[:], in0=ngm[:], scalar=rstd[:, 0:1], in1=b32[:], op0=ALU.mult, op1=ALU.add
+        )
+
+        for b in range(NB):
+            i = b
+            m = psum.tile([P, D], F32, name="r%d" % b, tag="m")
+            product(m[:], b, True, True)
+            o = outp.tile([P, D], F32, name="o%d" % b)
+            if b == 0:
+                for h in range(2):
+                    cols = slice(h * HALF, (h + 1) * HALF)
+                    nc.scalar.activation(
+                        out=o[:, cols], in_=m[:, cols], func=ACT.Relu, bias=shift[:, 0:1], scale=gain[:, 0:1]
+                    )
+                    nc.sync.dma_start(out=out[b, :, cols], in_=o[:, cols])
+                continue
+            if i % 3 != 1:
+                nc.scalar.activation(out=o[:], in_=m[:], func=ACT.Relu, bias=shift[:, 0:1], scale=gain[:, 0:1])
+            else:
+                nc.vector.tensor_scalar(
+                    out=o[:], in0=m[:], scalar1=gain[:, 0:1], scalar2=shift[:, 0:1], op0=ALU.mult, op1=ALU.add
+                )
+                nc.vector.tensor_scalar_max(out=o[:], in0=o[:], scalar1=0.0)
+            nc.sync.dma_start(out=out[b], in_=o[:])

@@ -7,6 +7,7 @@ FLOPS = 2 * 16 * 128 * 512 * 512
 
 F32 = mybir.dt.float32
 BF16 = mybir.dt.bfloat16
+I32 = mybir.dt.int32
 U32 = mybir.dt.uint32
 U8 = mybir.dt.uint8
 FP8X4 = mybir.dt.float8_e4m3fn_x4
@@ -19,14 +20,15 @@ NH = 4
 NB = 16
 D = 512
 EPS = 1e-5
-CHUNKS = [1] * 16
-CV = 336
-CV_LAST = 384
-MBUFS = 7
+NG = 3
+NU = 4 * NG
 HALF = 256
 PIV = 64
-MANUAL = True
-LAG_SWITCH = 99
+SQ = {5: (0,), 6: (1,), 7: (2,), 8: (3,), 9: (4,), 10: (5,), 11: (6,), 12: (7,), 13: (8, 9), 14: (10, 12), 15: (11, 13), 16: (14,)}
+SHARE = (256, 336, 416)
+BANK = (0, 1, 2, 3, 4, 5, 6, 0, 1, 2, 3, 4, 0, 5, 0, 5)
+KEPT = (8, 9, 10, 11, 6, 14, 15)
+AGAIN = (0, 1, 2, 3, 4, 5, 7, 12, 13)
 
 
 def tile_block_height_reducing_filtering_pb_t_kernel(tc, head_res, W_merge, g_m, b_m, out):
@@ -38,49 +40,64 @@ def tile_block_height_reducing_filtering_pb_t_kernel(tc, head_res, W_merge, g_m,
         codep = ctx.enter_context(tc.tile_pool(name="codep", bufs=1))
         outp = ctx.enter_context(tc.tile_pool(name="outp", bufs=1))
         small = ctx.enter_context(tc.tile_pool(name="small", bufs=1))
-        psum = ctx.enter_context(tc.psum_pool(name="psum", bufs=MBUFS))
-        if MANUAL:
-            ctx.enter_context(tc.manual_schedule())
+        psum = ctx.enter_context(tc.psum_pool(name="psum", bufs=1))
+        ctx.enter_context(tc.manual_schedule())
 
         w_sb = consts.tile([P, NH * P], BF16, name="w_sb")
-        nc.scalar.dma_start(out=w_sb[:], in_=W_merge)
+        nc.sync.dma_start(out=w_sb[:], in_=W_merge)
         g_bf = small.tile([P, 1], BF16, name="g_bf")
         b_bf = small.tile([P, 1], BF16, name="b_bf")
 
         raw_of = []
-        b0 = 0
-        for ci, nb in enumerate(CHUNKS):
-            raw = rawp.tile([P, nb, NH * D], BF16, name="raw%d" % ci)
-            for j in range(nb):
+        for u in range(NB):
+            raw = rawp.tile([P, NH * D], BF16, name="raw%d" % u)
+            if u < NU:
+                g, n = divmod(u, NH)
+                nc.sync.dma_start(
+                    out=raw[:], in_=head_res[n, 4 * g : 4 * g + 4].rearrange("b (q t) d -> (b q) (t d)", t=4)
+                )
+            else:
                 for n in (0, 2, 1, 3):
                     nc.sync.dma_start(
-                        out=raw[32 * n : 32 * n + 32, j, :],
-                        in_=head_res[n, b0 + j].rearrange("(q t) d -> q (t d)", t=4),
+                        out=raw[32 * n : 32 * n + 32, :], in_=head_res[n, u].rearrange("(q t) d -> q (t d)", t=4)
                     )
-            for j in range(nb):
-                raw_of.append((raw, j))
-            b0 += nb
+            raw_of.append(raw)
 
         one = small.tile([P, 1], F32, name="one")
         nc.vector.memset(one[:], 1.0)
         warm = small.tile([P, 1], F32, name="warm")
         nc.scalar.activation(out=warm[:], in_=one[:], func=ACT.Abs_reciprocal_sqrt)
-        ident = consts.tile([P, P], BF16, name="ident")
+        ident = consts.tile([P, P], F32, name="ident")
         make_identity(nc, ident[:])
+        planes = consts.tile([P, 5, NH * P], U8, name="planes", align_bytes=64)
+        nc.gpsimd.memset(planes[:].rearrange("p a b -> p (a b)").bitcast(I32), 0)
 
-        w_perm = consts.tile([P, 4, P], BF16, name="w_perm")
-        nc.vector.tensor_copy(out=w_perm[:], in_=w_sb[:].rearrange("o (p t) -> o t p", t=4))
-        wT_ps = psum.tile([P, 4, P], BF16, name="wT_ps", tag="m")
-        for t in range(4):
-            nc.tensor.transpose(wT_ps[:, t, :], w_perm[:, t, :], ident[:])
-        w_grp = consts.tile([P, P, 4], BF16, name="w_grp", align_bytes=64)
-        w_codes = consts.tile([P, P], U32, name="w_codes", align_bytes=64)
-        w_scales = consts.tile([P, P], U8, name="w_scales", align_bytes=64)
+        w_rep = consts.tile([P, NH, 4, P], BF16, name="w_rep")
+        for q in range(4):
+            nc.vector.tensor_copy(out=w_rep[:, :, q, :], in_=w_sb[:].rearrange("o (n x) -> o n x", n=NH))
+        rep_words = w_rep[:].rearrange("o n q x -> o (n q x)").bitcast(F32)
+        dir_words = w_sb[:].bitcast(F32)
+        wps = []
+        for i in range(2):
+            ps = psum.tile([P, 2, 2, P], F32, name="wps%d" % i, tag="bank%d" % i)
+            wps.append(ps)
+            for j in range(2):
+                for e in range(2):
+                    n = 2 * i + j
+                    nc.tensor.transpose(ps[:, j, e, :], rep_words[:, 256 * n + e : 256 * n + 256 : 2], ident[:])
+        wpd = psum.tile([P, 2, P], F32, name="wpd", tag="bank2")
+        for e in range(2):
+            nc.tensor.transpose(wpd[:, e, :], dir_words[:, e : 256 : 2], ident[:])
+        wr_grp = consts.tile([P, NH * P * 4], BF16, name="wr_grp", align_bytes=64)
+        wd_grp = consts.tile([P, P * 4], BF16, name="wd_grp", align_bytes=64)
+        wr_codes = consts.tile([P, NH * P], U32, name="wr_codes", align_bytes=64)
+        wd_codes = consts.tile([P, P], U32, name="wd_codes", align_bytes=64)
+        wd_scales = consts.tile([P, P], U8, name="wd_scales", align_bytes=64)
 
         g32 = small.tile([P, 1], F32, name="g32")
         b32 = small.tile([P, 1], F32, name="b32")
 
-        acc = psum.tile([P, D], F32, name="acc", tag="acc", bufs=1)
+        acc = psum.tile([P, D], F32, name="acc", tag="bank7")
         ss = small.tile([P, NB], F32, name="ss")
         junk = consts.tile([P, D], F32, name="junk")
         negc = small.tile([P, 1], F32, name="negc")
@@ -90,52 +107,67 @@ def tile_block_height_reducing_filtering_pb_t_kernel(tc, head_res, W_merge, g_m,
         scales_of = {}
         m_of = {}
 
-        def regroup_part(b, d0, d1):
-            raw, j = raw_of[b]
-            grp = grp_of[b]
-            src = raw[:, j, :].rearrange("p (t d) -> p t d", t=4)
-            dv = d0 + (d1 - d0) * (CV if b < NB - 3 else CV_LAST) // D
+        def regroup(u, dv):
+            grp = grpp.tile([P, D, 4], BF16, name="grp", align_bytes=64)
+            grp_of[u] = grp
+            src = raw_of[u][:].rearrange("p (t d) -> p t d", t=4)
             nc.vector.tensor_copy(
-                out=grp[:, d0:dv, :].rearrange("p (c i) t -> p c t i", i=4),
-                in_=src[:, :, d0:dv].rearrange("p t (c i) -> p c t i", i=4),
+                out=grp[:, 0:dv, :].rearrange("p (c i) t -> p c t i", i=4),
+                in_=src[:, :, 0:dv].rearrange("p t (c i) -> p c t i", i=4),
             )
             nc.scalar.copy(
-                out=grp[:, dv:d1, :].rearrange("p (c i) t -> p c t i", i=4),
-                in_=src[:, :, dv:d1].rearrange("p t (c i) -> p c t i", i=4),
+                out=grp[:, dv:D, :].rearrange("p (c i) t -> p c t i", i=4),
+                in_=src[:, :, dv:D].rearrange("p t (c i) -> p c t i", i=4),
             )
 
-        def regroup(b):
-            grp = grpp.tile([P, D, 4], BF16, name="grp", align_bytes=64)
-            grp_of[b] = grp
-            regroup_part(b, 0, D)
-
-        def quantise(b):
-            codes = codep.tile([P, D], U32, name="codes%d" % b, align_bytes=64)
-            scales = codep.tile([P, D], U8, name="scales%d" % b, align_bytes=64)
-            codes_of[b] = codes
-            scales_of[b] = scales
+        def quantise(u):
+            codes = codep.tile([P, D], U32, name="codes%d" % u, align_bytes=64)
+            scales = codep.tile([P, D], U8, name="scales%d" % u, align_bytes=64)
+            codes_of[u] = codes
+            scales_of[u] = scales
             nc.vector.quantize_mx(
                 out=codes[:].bitcast(FP8X4),
                 scales=scales[:],
-                in_=grp_of[b][:].rearrange("p d t -> p (d t)"),
+                in_=grp_of[u][:].rearrange("p d t -> p (d t)"),
             )
 
-        def product(dst, b, start, stop):
+        def mx_pass(dst, w_codes, w_scales, u, start, stop):
             nc.tensor.matmul_mx(
                 out=dst,
-                lhsT=w_codes[:].bitcast(FP8X4),
-                lhsT_scale=w_scales[:],
-                rhs=codes_of[b][:].bitcast(FP8X4),
-                rhs_scale=scales_of[b][:],
+                lhsT=w_codes.bitcast(FP8X4),
+                lhsT_scale=w_scales,
+                rhs=codes_of[u][:].bitcast(FP8X4),
+                rhs_scale=scales_of[u][:],
                 start=start,
                 stop=stop,
             )
 
-        def multiply(b):
-            product(acc[:], b, b == 0, b == NB - 1)
-            m = psum.tile([P, D], F32, name="m%d" % b, tag="m")
-            m_of[b] = m
-            product(m[:], b, True, True)
+        def head_pass(dst, plane, u, start, stop):
+            cols = slice(P * (u % NH), P * (u % NH) + P)
+            mx_pass(dst, wr_codes[:, cols], planes[:, plane, cols], u, start, stop)
+
+        def product(dst, b):
+            if b < NU:
+                for n in range(NH):
+                    head_pass(dst, b % 4, b - b % 4 + n, n == 0, n == NH - 1)
+            else:
+                mx_pass(dst, wd_codes[:], wd_scales[:], b, True, True)
+
+        def multiply(u):
+            if u < NU:
+                n = u % NH
+                for q in range(4):
+                    b = u - n + q
+                    if n == 0:
+                        m = psum.tile([P, D], F32, name="m%d" % b, tag="bank%d" % BANK[b])
+                        m_of[b] = m
+                    head_pass(m_of[b][:], q, u, n == 0, n == NH - 1)
+                head_pass(acc[:], 4, u, u == 0, False)
+            else:
+                m = psum.tile([P, D], F32, name="m%d" % u, tag="bank%d" % BANK[u])
+                m_of[u] = m
+                product(m[:], u)
+                mx_pass(acc[:], wd_codes[:], wd_scales[:], u, False, u == NB - 1)
 
         def squares(b):
             nc.scalar.activation(
@@ -143,21 +175,32 @@ def tile_block_height_reducing_filtering_pb_t_kernel(tc, head_res, W_merge, g_m,
                 accum_out=ss[:, b : b + 1],
             )
 
-        sq_next = 0
         for s in range(NB + 1):
             if s < NB:
-                regroup(s)
+                regroup(s, 384 if s == 0 else SHARE[len(SQ.get(s, ()))])
             if s == 0:
-                nc.scalar.copy(out=w_grp[:], in_=wT_ps[:].rearrange("p t o -> p o t"))
-            if s == 1:
-                nc.vector.quantize_mx(
-                    out=w_codes[:].bitcast(FP8X4), scales=w_scales[:],
-                    in_=w_grp[:].rearrange("p o t -> p (o t)"),
+                words = wr_grp[:].bitcast(F32).rearrange("p (n o e) -> p n o e", n=NH, e=2)
+                for i in range(2):
+                    nc.scalar.copy(out=words[:, 2 * i : 2 * i + 2], in_=wps[i][:].rearrange("p n e o -> p n o e"))
+                nc.scalar.copy(
+                    out=wd_grp[:].bitcast(F32).rearrange("p (o e) -> p o e", e=2),
+                    in_=wpd[:].rearrange("p e o -> p o e"),
                 )
+            if s == 1:
+                nc.vector.quantize_mx(out=wr_codes[:].bitcast(FP8X4), scales=planes[:, 4, :], in_=wr_grp[:])
             if s >= 1:
                 quantise(s - 1)
-                multiply(s - 1)
+            if s == 1:
+                for q in range(4):
+                    rows = slice(32 * q, 32 * q + 32)
+                    nc.vector.tensor_copy(
+                        out=planes[rows, q, :].bitcast(I32), in_=planes[rows, 4, :].bitcast(I32)
+                    )
             if s == 2:
+                nc.vector.quantize_mx(out=wd_codes[:].bitcast(FP8X4), scales=wd_scales[:], in_=wd_grp[:])
+            if s >= 1:
+                multiply(s - 1)
+            if s == 5:
                 nc.scalar.activation(
                     out=junk[:, 0:PIV], in_=m_of[0][:, 0:PIV], func=ACT.Identity, scale=-1.0 / PIV, accum_out=negc[:]
                 )
@@ -165,10 +208,8 @@ def tile_block_height_reducing_filtering_pb_t_kernel(tc, head_res, W_merge, g_m,
                 with nc.allow_non_contiguous_dma(reason="one gain and one shift per partition, 128 elements each"):
                     nc.scalar.dma_start(out=g_bf[:], in_=g_m.rearrange("(o u) -> o u", u=1))
                     nc.scalar.dma_start(out=b_bf[:], in_=b_m.rearrange("(o u) -> o u", u=1))
-            lag = 3 if s < LAG_SWITCH else 2
-            while sq_next <= s - lag:
-                squares(sq_next)
-                sq_next += 1
+            for b in SQ.get(s, ()):
+                squares(b)
         inv = 1.0 / (NB * D)
         ssp = small.tile([P, 1], F32, name="ssp")
         bias2 = small.tile([P, 1], F32, name="bias2")
@@ -186,9 +227,7 @@ def tile_block_height_reducing_filtering_pb_t_kernel(tc, head_res, W_merge, g_m,
         nc.vector.tensor_copy(out=b32[:], in_=b_bf[:])
         nc.vector.reduce_sum(out=ssp[:], in_=ss[:, 0 : NB - 2], axis=AX.X)
         nc.vector.tensor_scalar(out=bias2[:], in0=ssp[:], scalar1=inv, scalar2=EPS, op0=ALU.mult, op1=ALU.add)
-        while sq_next < NB:
-            squares(sq_next)
-            sq_next += 1
+        squares(NB - 1)
         nc.vector.reduce_sum(out=s1[:], in_=acc[:], axis=AX.X)
         nc.vector.tensor_scalar(out=dpos[:], in0=s1[:], scalar1=inv, scalar2=negc[:, 0:1], op0=ALU.mult, op1=ALU.add)
         nc.vector.tensor_scalar(
@@ -210,24 +249,38 @@ def tile_block_height_reducing_filtering_pb_t_kernel(tc, head_res, W_merge, g_m,
             out=shift[:], in0=ngm[:], scalar=rstd[:, 0:1], in1=b32[:], op0=ALU.mult, op1=ALU.add
         )
 
-        for b in range(NB):
-            i = b
-            m = psum.tile([P, D], F32, name="r%d" % b, tag="m")
-            product(m[:], b, True, True)
+        order = KEPT + AGAIN
+        bank_of = {}
+        for i, b in enumerate(KEPT):
+            bank_of[b] = BANK[b]
+        freed = [7] + [BANK[b] for b in KEPT] + [7]
+        for i, b in enumerate(AGAIN):
+            bank_of[b] = freed[i]
+
+        def remake(b):
+            m = psum.tile([P, D], F32, name="r%d" % b, tag="bank%d" % bank_of[b])
+            m_of[b] = m
+            product(m[:], b)
+
+        remake(AGAIN[0])
+        for i, b in enumerate(order):
+            m = m_of[b]
             o = outp.tile([P, D], F32, name="o%d" % b)
-            if b == 0:
+            if i == 0:
                 for h in range(2):
                     cols = slice(h * HALF, (h + 1) * HALF)
                     nc.scalar.activation(
                         out=o[:, cols], in_=m[:, cols], func=ACT.Relu, bias=shift[:, 0:1], scale=gain[:, 0:1]
                     )
                     nc.sync.dma_start(out=out[b, :, cols], in_=o[:, cols])
-                continue
-            if i % 3 != 1:
-                nc.scalar.activation(out=o[:], in_=m[:], func=ACT.Relu, bias=shift[:, 0:1], scale=gain[:, 0:1])
             else:
-                nc.vector.tensor_scalar(
-                    out=o[:], in0=m[:], scalar1=gain[:, 0:1], scalar2=shift[:, 0:1], op0=ALU.mult, op1=ALU.add
-                )
-                nc.vector.tensor_scalar_max(out=o[:], in0=o[:], scalar1=0.0)
-            nc.sync.dma_start(out=out[b], in_=o[:])
+                if i % 3 != 1:
+                    nc.scalar.activation(out=o[:], in_=m[:], func=ACT.Relu, bias=shift[:, 0:1], scale=gain[:, 0:1])
+                else:
+                    nc.vector.tensor_scalar(
+                        out=o[:], in0=m[:], scalar1=gain[:, 0:1], scalar2=shift[:, 0:1], op0=ALU.mult, op1=ALU.add
+                    )
+                    nc.vector.tensor_scalar_max(out=o[:], in0=o[:], scalar1=0.0)
+                nc.sync.dma_start(out=out[b], in_=o[:])
+            if i + 1 < len(AGAIN):
+                remake(AGAIN[i + 1])

@@ -24,11 +24,14 @@ NG = 3
 NU = 4 * NG
 HALF = 256
 PIV = 64
-SQ = {5: (0,), 6: (1,), 7: (2,), 8: (3,), 9: (4,), 10: (5,), 11: (6,), 12: (7,), 13: (8, 9), 14: (10, 12), 15: (11, 13), 16: (14,)}
-SHARE = (256, 336, 416)
-BANK = (0, 1, 2, 3, 4, 5, 6, 0, 1, 2, 3, 4, 0, 5, 0, 5)
-KEPT = (8, 9, 10, 11, 6, 14, 15)
-AGAIN = (0, 1, 2, 3, 4, 5, 7, 12, 13)
+SQ = {6: (0,), 7: (1, 2), 8: (3,), 9: (4,), 10: (5,), 11: (6,), 12: (7,), 13: (8, 9), 14: (10, 12), 15: (11, 13), 16: (14,)}
+SUMS = {6: 3, 7: 3, 8: 3, 9: 3, 10: 3, 11: 3, 12: 3, 13: 15, 14: 15, 15: 9}
+SHARE = (240, 336, 416)
+EARLY = {0: 352, 1: 208}
+BANK = (0, 1, 2, 3, 4, 5, 6, 0, 1, 2, 3, 4, 0, 6, 0)
+BANK_LAST = (6, 0)
+KEPT = (8, 9, 10, 11, 5)
+AGAIN = (0, 12, 13, 14, 1, 2, 3, 4, 6, 7)
 
 
 def tile_block_height_reducing_filtering_pb_t_kernel(tc, head_res, W_merge, g_m, b_m, out):
@@ -73,8 +76,10 @@ def tile_block_height_reducing_filtering_pb_t_kernel(tc, head_res, W_merge, g_m,
         nc.gpsimd.memset(planes[:].rearrange("p a b -> p (a b)").bitcast(I32), 0)
 
         w_rep = consts.tile([P, NH, 4, P], BF16, name="w_rep")
-        for q in range(4):
-            nc.vector.tensor_copy(out=w_rep[:, :, q, :], in_=w_sb[:].rearrange("o (n x) -> o n x", n=NH))
+        for n in range(NH):
+            nc.vector.tensor_copy(
+                out=w_rep[:, n], in_=w_sb[:, P * n : P * n + P].unsqueeze(1).to_broadcast([P, 4, P])
+            )
         rep_words = w_rep[:].rearrange("o n q x -> o (n q x)").bitcast(F32)
         dir_words = w_sb[:].bitcast(F32)
         wps = []
@@ -97,8 +102,8 @@ def tile_block_height_reducing_filtering_pb_t_kernel(tc, head_res, W_merge, g_m,
         g32 = small.tile([P, 1], F32, name="g32")
         b32 = small.tile([P, 1], F32, name="b32")
 
-        acc = psum.tile([P, D], F32, name="acc", tag="bank7")
-        ss = small.tile([P, NB], F32, name="ss")
+        acc = psum.tile([P, P], F32, name="acc", tag="bank7")
+        ss = small.tile([P, NB + 1], F32, name="ss")
         junk = consts.tile([P, D], F32, name="junk")
         negc = small.tile([P, 1], F32, name="negc")
 
@@ -115,29 +120,31 @@ def tile_block_height_reducing_filtering_pb_t_kernel(tc, head_res, W_merge, g_m,
                 out=grp[:, 0:dv, :].rearrange("p (c i) t -> p c t i", i=4),
                 in_=src[:, :, 0:dv].rearrange("p t (c i) -> p c t i", i=4),
             )
-            nc.scalar.copy(
-                out=grp[:, dv:D, :].rearrange("p (c i) t -> p c t i", i=4),
-                in_=src[:, :, dv:D].rearrange("p t (c i) -> p c t i", i=4),
-            )
+            if dv < D:
+                nc.scalar.copy(
+                    out=grp[:, dv:D, :].rearrange("p (c i) t -> p c t i", i=4),
+                    in_=src[:, :, dv:D].rearrange("p t (c i) -> p c t i", i=4),
+                )
 
-        def quantise(u):
-            codes = codep.tile([P, D], U32, name="codes%d" % u, align_bytes=64)
-            scales = codep.tile([P, D], U8, name="scales%d" % u, align_bytes=64)
-            codes_of[u] = codes
-            scales_of[u] = scales
+        def quantise(u, cols=slice(0, D)):
+            if u not in codes_of:
+                codes = codep.tile([P, D], U32, name="codes%d" % u, align_bytes=64)
+                scales = codep.tile([P, D], U8, name="scales%d" % u, align_bytes=64)
+                codes_of[u] = codes
+                scales_of[u] = scales
             nc.vector.quantize_mx(
-                out=codes[:].bitcast(FP8X4),
-                scales=scales[:],
-                in_=grp_of[u][:].rearrange("p d t -> p (d t)"),
+                out=codes_of[u][:, cols].bitcast(FP8X4),
+                scales=scales_of[u][:, cols],
+                in_=grp_of[u][:, cols].rearrange("p d t -> p (d t)"),
             )
 
-        def mx_pass(dst, w_codes, w_scales, u, start, stop):
+        def mx_pass(dst, w_codes, w_scales, u, start, stop, cols=slice(0, D)):
             nc.tensor.matmul_mx(
                 out=dst,
                 lhsT=w_codes.bitcast(FP8X4),
                 lhsT_scale=w_scales,
-                rhs=codes_of[u][:].bitcast(FP8X4),
-                rhs_scale=scales_of[u][:],
+                rhs=codes_of[u][:, cols].bitcast(FP8X4),
+                rhs_scale=scales_of[u][:, cols],
                 start=start,
                 stop=stop,
             )
@@ -153,54 +160,77 @@ def tile_block_height_reducing_filtering_pb_t_kernel(tc, head_res, W_merge, g_m,
             else:
                 mx_pass(dst, wd_codes[:], wd_scales[:], b, True, True)
 
+        def new_m(b):
+            m = psum.tile([P, D], F32, name="m%d" % b, tag="bank%d" % BANK[b])
+            m_of[b] = m
+
         def multiply(u):
             if u < NU:
                 n = u % NH
+                first = u - n
                 for q in range(4):
-                    b = u - n + q
-                    if n == 0:
-                        m = psum.tile([P, D], F32, name="m%d" % b, tag="bank%d" % BANK[b])
-                        m_of[b] = m
-                    head_pass(m_of[b][:], q, u, n == 0, n == NH - 1)
-                head_pass(acc[:], 4, u, u == 0, False)
+                    for k in ((n,) if q < 3 or n > 1 else range(2 * n)):
+                        if k == 0:
+                            new_m(first + q)
+                        head_pass(m_of[first + q][:], q, first + k, k == 0, k == NH - 1)
             else:
-                m = psum.tile([P, D], F32, name="m%d" % u, tag="bank%d" % BANK[u])
-                m_of[u] = m
-                product(m[:], u)
-                mx_pass(acc[:], wd_codes[:], wd_scales[:], u, False, u == NB - 1)
+                new_m(u)
+                product(m_of[u][:], u)
 
-        def squares(b):
+        sums_done = []
+
+        def add_sums(count):
+            for i in range(len(sums_done), len(sums_done) + count):
+                u, c = divmod(i, 4)
+                cols_w = slice(P * (u % NH), P * (u % NH) + P)
+                w_codes, w_scales = (
+                    (wr_codes[:, cols_w], planes[:, 4, cols_w]) if u < NU else (wd_codes[:], wd_scales[:])
+                )
+                mx_pass(acc[:], w_codes, w_scales, u, i == 0, i == 4 * NB - 1, slice(P * c, P * c + P))
+                sums_done.append(i)
+
+        def squares(m, i):
             nc.scalar.activation(
-                out=junk[:], in_=m_of[b][:], func=ACT.Square, bias=negc[:, 0:1], scale=1.0,
-                accum_out=ss[:, b : b + 1],
+                out=junk[:, 0 : m.shape[1]], in_=m, func=ACT.Square, bias=negc[:, 0:1], scale=1.0,
+                accum_out=ss[:, i : i + 1],
             )
 
+        halves = (slice(0, HALF), slice(HALF, D))
+        m_last = []
         for s in range(NB + 1):
             if s < NB:
-                regroup(s, 384 if s == 0 else SHARE[len(SQ.get(s, ()))])
+                regroup(s, EARLY.get(s, SHARE[len(SQ.get(s, ()))]))
             if s == 0:
                 words = wr_grp[:].bitcast(F32).rearrange("p (n o e) -> p n o e", n=NH, e=2)
-                for i in range(2):
-                    nc.scalar.copy(out=words[:, 2 * i : 2 * i + 2], in_=wps[i][:].rearrange("p n e o -> p n o e"))
-                nc.scalar.copy(
-                    out=wd_grp[:].bitcast(F32).rearrange("p (o e) -> p o e", e=2),
-                    in_=wpd[:].rearrange("p e o -> p o e"),
-                )
-            if s == 1:
+                nc.scalar.copy(out=words[:, 0:2], in_=wps[0][:].rearrange("p n e o -> p n o e"))
+                quantise(0)
+                nc.vector.tensor_copy(out=words[:, 2:4], in_=wps[1][:].rearrange("p n e o -> p n o e"))
                 nc.vector.quantize_mx(out=wr_codes[:].bitcast(FP8X4), scales=planes[:, 4, :], in_=wr_grp[:])
-            if s >= 1:
-                quantise(s - 1)
-            if s == 1:
                 for q in range(4):
                     rows = slice(32 * q, 32 * q + 32)
                     nc.vector.tensor_copy(
                         out=planes[rows, q, :].bitcast(I32), in_=planes[rows, 4, :].bitcast(I32)
                     )
-            if s == 2:
+            if s == 1:
+                nc.scalar.copy(
+                    out=wd_grp[:].bitcast(F32).rearrange("p (o e) -> p o e", e=2),
+                    in_=wpd[:].rearrange("p e o -> p o e"),
+                )
+            if 2 <= s < NB:
+                quantise(s - 1)
+            if s == 3:
                 nc.vector.quantize_mx(out=wd_codes[:].bitcast(FP8X4), scales=wd_scales[:], in_=wd_grp[:])
-            if s >= 1:
+            if 1 <= s < NB:
                 multiply(s - 1)
-            if s == 5:
+            add_sums(SUMS.get(s, 0))
+            if s == NB:
+                for h in range(2):
+                    quantise(NB - 1, halves[h])
+                    m = psum.tile([P, HALF], F32, name="m%d_%d" % (NB - 1, h), tag="bank%d" % BANK_LAST[h])
+                    m_last.append(m)
+                    mx_pass(m[:], wd_codes[:], wd_scales[:], NB - 1, True, True, halves[h])
+                    add_sums(2)
+            if s == 6:
                 nc.scalar.activation(
                     out=junk[:, 0:PIV], in_=m_of[0][:, 0:PIV], func=ACT.Identity, scale=-1.0 / PIV, accum_out=negc[:]
                 )
@@ -209,78 +239,81 @@ def tile_block_height_reducing_filtering_pb_t_kernel(tc, head_res, W_merge, g_m,
                     nc.scalar.dma_start(out=g_bf[:], in_=g_m.rearrange("(o u) -> o u", u=1))
                     nc.scalar.dma_start(out=b_bf[:], in_=b_m.rearrange("(o u) -> o u", u=1))
             for b in SQ.get(s, ()):
-                squares(b)
+                squares(m_of[b][:], b)
+            if s == NB - 1:
+                nc.vector.tensor_copy(out=g32[:], in_=g_bf[:])
+                nc.vector.tensor_copy(out=b32[:], in_=b_bf[:])
         inv = 1.0 / (NB * D)
         ssp = small.tile([P, 1], F32, name="ssp")
-        bias2 = small.tile([P, 1], F32, name="bias2")
-        bias2b = small.tile([P, 1], F32, name="bias2b")
+        part = []
+        for i in range(3):
+            p_ = small.tile([P, 1], F32, name="part%d" % i)
+            part.append(p_)
         s1 = small.tile([P, 1], F32, name="s1")
-        dpos = small.tile([P, 1], F32, name="dpos")
-        dneg = small.tile([P, 1], F32, name="dneg")
+        delta = small.tile([P, 1], F32, name="delta")
+        negv = small.tile([P, 1], F32, name="negv")
         nmean = small.tile([P, 1], F32, name="nmean")
         ngm = small.tile([P, 1], F32, name="ngm")
-        bias3 = small.tile([P, 1], F32, name="bias3")
         rstd = small.tile([P, 1], F32, name="rstd")
         gain = small.tile([P, 1], F32, name="gain")
+        gain_v = small.tile([P, 1], F32, name="gain_v")
         shift = small.tile([P, 1], F32, name="shift")
-        nc.vector.tensor_copy(out=g32[:], in_=g_bf[:])
-        nc.vector.tensor_copy(out=b32[:], in_=b_bf[:])
         nc.vector.reduce_sum(out=ssp[:], in_=ss[:, 0 : NB - 2], axis=AX.X)
-        nc.vector.tensor_scalar(out=bias2[:], in0=ssp[:], scalar1=inv, scalar2=EPS, op0=ALU.mult, op1=ALU.add)
-        squares(NB - 1)
+        nc.vector.tensor_scalar(out=part[0][:], in0=ssp[:], scalar1=inv, scalar2=EPS, op0=ALU.mult, op1=ALU.add)
+        for h in range(2):
+            squares(m_last[h][:], NB - 1 + h)
+        for i in range(2):
+            nc.vector.scalar_tensor_tensor(
+                out=part[i + 1][:], in0=ss[:, NB - 2 + i : NB - 1 + i], scalar=inv, in1=part[i][:],
+                op0=ALU.mult, op1=ALU.add,
+            )
         nc.vector.reduce_sum(out=s1[:], in_=acc[:], axis=AX.X)
-        nc.vector.tensor_scalar(out=dpos[:], in0=s1[:], scalar1=inv, scalar2=negc[:, 0:1], op0=ALU.mult, op1=ALU.add)
-        nc.vector.tensor_scalar(
-            out=dneg[:], in0=s1[:], scalar1=-inv, scalar2=negc[:, 0:1], op0=ALU.mult, op1=ALU.subtract
-        )
+        nc.vector.tensor_scalar(out=delta[:], in0=s1[:], scalar1=inv, scalar2=negc[:, 0:1], op0=ALU.mult, op1=ALU.add)
         nc.vector.scalar_tensor_tensor(
-            out=bias2b[:], in0=ss[:, NB - 2 : NB - 1], scalar=inv, in1=bias2[:], op0=ALU.mult, op1=ALU.add
-        )
-        nc.vector.scalar_tensor_tensor(
-            out=bias3[:], in0=dpos[:], scalar=dneg[:, 0:1], in1=bias2b[:], op0=ALU.mult, op1=ALU.add
-        )
-        nc.scalar.activation(
-            out=rstd[:], in_=ss[:, NB - 1 : NB], func=ACT.Abs_reciprocal_sqrt, bias=bias3[:, 0:1], scale=inv
+            out=negv[:], in0=delta[:], scalar=delta[:, 0:1], in1=part[2][:], op0=ALU.mult, op1=ALU.subtract
         )
         nc.vector.tensor_scalar(out=nmean[:], in0=s1[:], scalar1=-inv, scalar2=None, op0=ALU.mult)
         nc.vector.tensor_tensor(out=ngm[:], in0=nmean[:], in1=g32[:], op=ALU.mult)
-        nc.vector.tensor_tensor(out=gain[:], in0=g32[:], in1=rstd[:], op=ALU.mult)
+        nc.scalar.activation(
+            out=rstd[:], in_=ss[:, NB : NB + 1], func=ACT.Abs_reciprocal_sqrt, bias=negv[:, 0:1], scale=-inv
+        )
+        nc.scalar.activation(out=gain[:], in_=rstd[:], func=ACT.Copy, scale=g32[:, 0:1])
         nc.vector.scalar_tensor_tensor(
             out=shift[:], in0=ngm[:], scalar=rstd[:, 0:1], in1=b32[:], op0=ALU.mult, op1=ALU.add
         )
+        nc.vector.tensor_tensor(out=gain_v[:], in0=g32[:], in1=rstd[:], op=ALU.mult)
 
-        order = KEPT + AGAIN
-        bank_of = {}
-        for i, b in enumerate(KEPT):
-            bank_of[b] = BANK[b]
-        freed = [7] + [BANK[b] for b in KEPT] + [7]
-        for i, b in enumerate(AGAIN):
-            bank_of[b] = freed[i]
+        freed = (7,) + BANK_LAST + tuple(BANK[b] for b in KEPT) + (7,) + BANK_LAST
 
-        def remake(b):
-            m = psum.tile([P, D], F32, name="r%d" % b, tag="bank%d" % bank_of[b])
+        def remake(i):
+            b = AGAIN[i]
+            m = psum.tile([P, D], F32, name="r%d" % b, tag="bank%d" % freed[i])
             m_of[b] = m
             product(m[:], b)
 
-        remake(AGAIN[0])
-        for i, b in enumerate(order):
-            m = m_of[b]
+        def on_scalar(dst, m):
+            nc.scalar.activation(out=dst, in_=m, func=ACT.Relu, bias=shift[:, 0:1], scale=gain[:, 0:1])
+
+        def on_vector(dst, m):
+            nc.vector.tensor_scalar(
+                out=dst, in0=m, scalar1=gain_v[:, 0:1], scalar2=shift[:, 0:1], op0=ALU.mult, op1=ALU.add
+            )
+            nc.vector.tensor_scalar_max(out=dst, in0=dst, scalar1=0.0)
+
+        remake(0)
+        o = outp.tile([P, D], F32, name="o%d" % (NB - 1))
+        on_scalar(o[:, halves[0]], m_last[0][:])
+        on_vector(o[:, halves[1]], m_last[1][:])
+        for h in range(2):
+            nc.sync.dma_start(out=out[NB - 1, :, halves[h]], in_=o[:, halves[h]])
+        remake(1)
+        remake(2)
+        for i, b in enumerate(KEPT + AGAIN):
             o = outp.tile([P, D], F32, name="o%d" % b)
-            if i == 0:
-                for h in range(2):
-                    cols = slice(h * HALF, (h + 1) * HALF)
-                    nc.scalar.activation(
-                        out=o[:, cols], in_=m[:, cols], func=ACT.Relu, bias=shift[:, 0:1], scale=gain[:, 0:1]
-                    )
-                    nc.sync.dma_start(out=out[b, :, cols], in_=o[:, cols])
+            if i % 3 != 1:
+                on_scalar(o[:], m_of[b][:])
             else:
-                if i % 3 != 1:
-                    nc.scalar.activation(out=o[:], in_=m[:], func=ACT.Relu, bias=shift[:, 0:1], scale=gain[:, 0:1])
-                else:
-                    nc.vector.tensor_scalar(
-                        out=o[:], in0=m[:], scalar1=gain[:, 0:1], scalar2=shift[:, 0:1], op0=ALU.mult, op1=ALU.add
-                    )
-                    nc.vector.tensor_scalar_max(out=o[:], in0=o[:], scalar1=0.0)
-                nc.sync.dma_start(out=out[b], in_=o[:])
-            if i + 1 < len(AGAIN):
-                remake(AGAIN[i + 1])
+                on_vector(o[:], m_of[b][:])
+            nc.sync.dma_start(out=out[b], in_=o[:])
+            if i + 3 < len(AGAIN):
+                remake(i + 3)

@@ -25,9 +25,9 @@ NU = 4 * NG
 HALF = 256
 PIV = 64
 SQ = {6: (0,), 7: (1, 2), 8: (3,), 9: (4,), 10: (5,), 11: (6,), 12: (7,), 13: (8, 9), 14: (10, 12), 15: (11, 13), 16: (14,)}
-SUMS = {6: 3, 7: 3, 8: 3, 9: 3, 10: 3, 11: 3, 12: 3, 13: 15, 14: 15, 15: 9}
-SHARE = (240, 336, 416)
-EARLY = {0: 352, 1: 208}
+SUMS = {4: 1, 5: 1, 6: 1, 7: 1, 8: 1, 9: 1, 10: 1, 11: 1, 12: 1, 13: 8, 14: 8, 15: 5}
+SHARE = (224, 336, 416)
+EARLY = {0: 512, 1: 176}
 BANK = (0, 1, 2, 3, 4, 5, 6, 0, 1, 2, 3, 4, 0, 6, 0)
 BANK_LAST = (6, 0)
 KEPT = (8, 9, 10, 11, 5)
@@ -93,6 +93,11 @@ def tile_block_height_reducing_filtering_pb_t_kernel(tc, head_res, W_merge, g_m,
         wpd = psum.tile([P, 2, P], F32, name="wpd", tag="bank2")
         for e in range(2):
             nc.tensor.transpose(wpd[:, e, :], dir_words[:, e : 256 : 2], ident[:])
+        warm_ps = psum.tile([P, D], F32, name="warm_ps", tag="bank3")
+        for i in range(5):
+            nc.tensor.matmul(
+                warm_ps[:], lhsT=w_sb[:, 0:P], rhs=w_rep[:, 0].rearrange("o q x -> o (q x)"), start=True, stop=True
+            )
         wr_grp = consts.tile([P, NH * P * 4], BF16, name="wr_grp", align_bytes=64)
         wd_grp = consts.tile([P, P * 4], BF16, name="wd_grp", align_bytes=64)
         wr_codes = consts.tile([P, NH * P], U32, name="wr_codes", align_bytes=64)
@@ -102,7 +107,7 @@ def tile_block_height_reducing_filtering_pb_t_kernel(tc, head_res, W_merge, g_m,
         g32 = small.tile([P, 1], F32, name="g32")
         b32 = small.tile([P, 1], F32, name="b32")
 
-        acc = psum.tile([P, P], F32, name="acc", tag="bank7")
+        acc = psum.tile([P, HALF], F32, name="acc", tag="bank7")
         ss = small.tile([P, NB + 1], F32, name="ss")
         junk = consts.tile([P, D], F32, name="junk")
         negc = small.tile([P, 1], F32, name="negc")
@@ -177,16 +182,17 @@ def tile_block_height_reducing_filtering_pb_t_kernel(tc, head_res, W_merge, g_m,
                 new_m(u)
                 product(m_of[u][:], u)
 
+        halves = (slice(0, HALF), slice(HALF, D))
         sums_done = []
 
         def add_sums(count):
             for i in range(len(sums_done), len(sums_done) + count):
-                u, c = divmod(i, 4)
+                u, h = divmod(i, 2)
                 cols_w = slice(P * (u % NH), P * (u % NH) + P)
                 w_codes, w_scales = (
                     (wr_codes[:, cols_w], planes[:, 4, cols_w]) if u < NU else (wd_codes[:], wd_scales[:])
                 )
-                mx_pass(acc[:], w_codes, w_scales, u, i == 0, i == 4 * NB - 1, slice(P * c, P * c + P))
+                mx_pass(acc[:], w_codes, w_scales, u, i == 0, i == 2 * NB - 1, halves[h])
                 sums_done.append(i)
 
         def squares(m, i):
@@ -195,16 +201,15 @@ def tile_block_height_reducing_filtering_pb_t_kernel(tc, head_res, W_merge, g_m,
                 accum_out=ss[:, i : i + 1],
             )
 
-        halves = (slice(0, HALF), slice(HALF, D))
         m_last = []
         for s in range(NB + 1):
             if s < NB:
                 regroup(s, EARLY.get(s, SHARE[len(SQ.get(s, ()))]))
             if s == 0:
                 words = wr_grp[:].bitcast(F32).rearrange("p (n o e) -> p n o e", n=NH, e=2)
-                nc.scalar.copy(out=words[:, 0:2], in_=wps[0][:].rearrange("p n e o -> p n o e"))
+                for i in range(2):
+                    nc.scalar.copy(out=words[:, 2 * i : 2 * i + 2], in_=wps[i][:].rearrange("p n e o -> p n o e"))
                 quantise(0)
-                nc.vector.tensor_copy(out=words[:, 2:4], in_=wps[1][:].rearrange("p n e o -> p n o e"))
                 nc.vector.quantize_mx(out=wr_codes[:].bitcast(FP8X4), scales=planes[:, 4, :], in_=wr_grp[:])
                 for q in range(4):
                     rows = slice(32 * q, 32 * q + 32)
@@ -229,7 +234,7 @@ def tile_block_height_reducing_filtering_pb_t_kernel(tc, head_res, W_merge, g_m,
                     m = psum.tile([P, HALF], F32, name="m%d_%d" % (NB - 1, h), tag="bank%d" % BANK_LAST[h])
                     m_last.append(m)
                     mx_pass(m[:], wd_codes[:], wd_scales[:], NB - 1, True, True, halves[h])
-                    add_sums(2)
+                    add_sums(1)
             if s == 6:
                 nc.scalar.activation(
                     out=junk[:, 0:PIV], in_=m_of[0][:, 0:PIV], func=ACT.Identity, scale=-1.0 / PIV, accum_out=negc[:]

@@ -66,6 +66,10 @@ def tile_block_height_reducing_filtering_pb_t_kernel(tc, head_res, W_merge, g_m,
                     )
             raw_of.append(raw)
 
+        with nc.allow_non_contiguous_dma(reason="one gain and one shift per partition, 128 elements each"):
+            nc.sync.dma_start(out=g_bf[:], in_=g_m.rearrange("(o u) -> o u", u=1))
+            nc.sync.dma_start(out=b_bf[:], in_=b_m.rearrange("(o u) -> o u", u=1))
+
         one = small.tile([P, 1], F32, name="one")
         nc.vector.memset(one[:], 1.0)
         warm = small.tile([P, 1], F32, name="warm")
@@ -239,15 +243,8 @@ def tile_block_height_reducing_filtering_pb_t_kernel(tc, head_res, W_merge, g_m,
                 nc.scalar.activation(
                     out=junk[:, 0:PIV], in_=m_of[0][:, 0:PIV], func=ACT.Identity, scale=-1.0 / PIV, accum_out=negc[:]
                 )
-            if s == 12:
-                with nc.allow_non_contiguous_dma(reason="one gain and one shift per partition, 128 elements each"):
-                    nc.scalar.dma_start(out=g_bf[:], in_=g_m.rearrange("(o u) -> o u", u=1))
-                    nc.scalar.dma_start(out=b_bf[:], in_=b_m.rearrange("(o u) -> o u", u=1))
             for b in SQ.get(s, ()):
                 squares(m_of[b][:], b)
-            if s == NB - 1:
-                nc.vector.tensor_copy(out=g32[:], in_=g_bf[:])
-                nc.vector.tensor_copy(out=b32[:], in_=b_bf[:])
         inv = 1.0 / (NB * D)
         ssp = small.tile([P, 1], F32, name="ssp")
         part = []
@@ -277,6 +274,8 @@ def tile_block_height_reducing_filtering_pb_t_kernel(tc, head_res, W_merge, g_m,
         nc.vector.scalar_tensor_tensor(
             out=negv[:], in0=delta[:], scalar=delta[:, 0:1], in1=part[2][:], op0=ALU.mult, op1=ALU.subtract
         )
+        nc.vector.tensor_copy(out=g32[:], in_=g_bf[:])
+        nc.vector.tensor_copy(out=b32[:], in_=b_bf[:])
         nc.vector.tensor_scalar(out=nmean[:], in0=s1[:], scalar1=-inv, scalar2=None, op0=ALU.mult)
         nc.vector.tensor_tensor(out=ngm[:], in0=nmean[:], in1=g32[:], op=ALU.mult)
         nc.scalar.activation(

from contextlib import ExitStack

import concourse.mybir as mybir
from concourse.masks import make_identity

FLOPS = 2 * 16 * 128 * 512 * 512

F32 = mybir.dt.float32
BF16 = mybir.dt.bfloat16
I32 = mybir.dt.int32
U32 = mybir.dt.uint32
U8 = mybir.dt.uint8
FP8X4 = mybir.dt.float8_e4m3fn_x4
ALU = mybir.AluOpType
ACT = mybir.ActivationFunctionType
AX = mybir.AxisListType

P = 128
NH = 4
NB = 16
D = 512
EPS = 1e-5
NG = 3
NU = 4 * NG
HALF = 256
PIV = 64
SQ = {6: (0,), 7: (1, 2), 8: (3,), 9: (4,), 10: (5,), 11: (6,), 12: (7,), 13: (8, 9), 14: (10, 12), 15: (11, 13), 16: (14,)}
SUMS = {4: 1, 5: 1, 6: 1, 7: 1, 8: 1, 9: 1, 10: 1, 11: 1, 12: 1, 13: 8, 14: 8, 15: 5}
SHARE = (224, 336, 416)
EARLY = {0: 512, 1: 176}
BANK = (0, 1, 2, 3, 4, 5, 6, 0, 1, 2, 3, 4, 0, 6, 0)
BANK_LAST = (6, 0)
KEPT = (8, 9, 10, 11, 5)
AGAIN = (0, 12, 13, 14, 1, 2, 3, 4, 6, 7)


def tile_block_height_reducing_filtering_pb_t_kernel(tc, head_res, W_merge, g_m, b_m, out):
    nc = tc.nc
    with ExitStack() as ctx:
        consts = ctx.enter_context(tc.tile_pool(name="consts", bufs=1))
        rawp = ctx.enter_context(tc.tile_pool(name="rawp", bufs=1))
        grpp = ctx.enter_context(tc.tile_pool(name="grpp", bufs=4))
        codep = ctx.enter_context(tc.tile_pool(name="codep", bufs=1))
        outp = ctx.enter_context(tc.tile_pool(name="outp", bufs=1))
        small = ctx.enter_context(tc.tile_pool(name="small", bufs=1))
        psum = ctx.enter_context(tc.psum_pool(name="psum", bufs=1))
        ctx.enter_context(tc.manual_schedule())

        w_sb = consts.tile([P, NH * P], BF16, name="w_sb")
        nc.sync.dma_start(out=w_sb[:], in_=W_merge)
        g_bf = small.tile([P, 1], BF16, name="g_bf")
        b_bf = small.tile([P, 1], BF16, name="b_bf")

        raw_of = []
        for u in range(NB):
            raw = rawp.tile([P, NH * D], BF16, name="raw%d" % u)
            if u < NU:
                g, n = divmod(u, NH)
                nc.sync.dma_start(
                    out=raw[:], in_=head_res[n, 4 * g : 4 * g + 4].rearrange("b (q t) d -> (b q) (t d)", t=4)
                )
            else:
                for n in (0, 2, 1, 3):
                    nc.sync.dma_start(
                        out=raw[32 * n : 32 * n + 32, :], in_=head_res[n, u].rearrange("(q t) d -> q (t d)", t=4)
                    )
            raw_of.append(raw)

        with nc.allow_non_contiguous_dma(reason="one gain and one shift per partition, 128 elements each"):
            nc.sync.dma_start(out=g_bf[:], in_=g_m.rearrange("(o u) -> o u", u=1))
            nc.sync.dma_start(out=b_bf[:], in_=b_m.rearrange("(o u) -> o u", u=1))

        one = small.tile([P, 1], F32, name="one")
        nc.vector.memset(one[:], 1.0)
        warm = small.tile([P, 1], F32, name="warm")
        nc.scalar.activation(out=warm[:], in_=one[:], func=ACT.Abs_reciprocal_sqrt)
        ident = consts.tile([P, P], F32, name="ident")
        make_identity(nc, ident[:])
        planes = consts.tile([P, 5, NH * P], U8, name="planes", align_bytes=64)
        nc.gpsimd.memset(planes[:].rearrange("p a b -> p (a b)").bitcast(I32), 0)

        w_rep = consts.tile([P, NH, 4, P], BF16, name="w_rep")
        for n in range(NH):
            nc.vector.tensor_copy(
                out=w_rep[:, n], in_=w_sb[:, P * n : P * n + P].unsqueeze(1).to_broadcast([P, 4, P])
            )
        rep_words = w_rep[:].rearrange("o n q x -> o (n q x)").bitcast(F32)
        dir_words = w_sb[:].bitcast(F32)
        wps = []
        for i in range(2):
            ps = psum.tile([P, 2, 2, P], F32, name="wps%d" % i, tag="bank%d" % i)
            wps.append(ps)
            for j in range(2):
                for e in range(2):
                    n = 2 * i + j
                    nc.tensor.transpose(ps[:, j, e, :], rep_words[:, 256 * n + e : 256 * n + 256 : 2], ident[:])
        wpd = psum.tile([P, 2, P], F32, name="wpd", tag="bank2")
        for e in range(2):
            nc.tensor.transpose(wpd[:, e, :], dir_words[:, e : 256 : 2], ident[:])
        warm_ps = psum.tile([P, D], F32, name="warm_ps", tag="bank3")
        for i in range(5):
            nc.tensor.matmul(
                warm_ps[:], lhsT=w_sb[:, 0:P], rhs=w_rep[:, 0].rearrange("o q x -> o (q x)"), start=True, stop=True
            )
        wr_grp = consts.tile([P, NH * P * 4], BF16, name="wr_grp", align_bytes=64)
        wd_grp = consts.tile([P, P * 4], BF16, name="wd_grp", align_bytes=64)
        wr_codes = consts.tile([P, NH * P], U32, name="wr_codes", align_bytes=64)
        wd_codes = consts.tile([P, P], U32, name="wd_codes", align_bytes=64)
        wd_scales = consts.tile([P, P], U8, name="wd_scales", align_bytes=64)

        g32 = small.tile([P, 1], F32, name="g32")
        b32 = small.tile([P, 1], F32, name="b32")

        acc = psum.tile([P, HALF], F32, name="acc", tag="bank7")
        ss = small.tile([P, NB + 1], F32, name="ss")
        junk = consts.tile([P, D], F32, name="junk")
        negc = small.tile([P, 1], F32, name="negc")

        grp_of = {}
        codes_of = {}
        scales_of = {}
        m_of = {}

        def regroup(u, dv):
            grp = grpp.tile([P, D, 4], BF16, name="grp", align_bytes=64)
            grp_of[u] = grp
            src = raw_of[u][:].rearrange("p (t d) -> p t d", t=4)
            nc.vector.tensor_copy(
                out=grp[:, 0:dv, :].rearrange("p (c i) t -> p c t i", i=4),
                in_=src[:, :, 0:dv].rearrange("p t (c i) -> p c t i", i=4),
            )
            if dv < D:
                nc.scalar.copy(
                    out=grp[:, dv:D, :].rearrange("p (c i) t -> p c t i", i=4),
                    in_=src[:, :, dv:D].rearrange("p t (c i) -> p c t i", i=4),
                )

        def quantise(u, cols=slice(0, D)):
            if u not in codes_of:
                codes = codep.tile([P, D], U32, name="codes%d" % u, align_bytes=64)
                scales = codep.tile([P, D], U8, name="scales%d" % u, align_bytes=64)
                codes_of[u] = codes
                scales_of[u] = scales
            nc.vector.quantize_mx(
                out=codes_of[u][:, cols].bitcast(FP8X4),
                scales=scales_of[u][:, cols],
                in_=grp_of[u][:, cols].rearrange("p d t -> p (d t)"),
            )

        def mx_pass(dst, w_codes, w_scales, u, start, stop, cols=slice(0, D)):
            nc.tensor.matmul_mx(
                out=dst,
                lhsT=w_codes.bitcast(FP8X4),
                lhsT_scale=w_scales,
                rhs=codes_of[u][:, cols].bitcast(FP8X4),
                rhs_scale=scales_of[u][:, cols],
                start=start,
                stop=stop,
            )

        def head_pass(dst, plane, u, start, stop):
            cols = slice(P * (u % NH), P * (u % NH) + P)
            mx_pass(dst, wr_codes[:, cols], planes[:, plane, cols], u, start, stop)

        def product(dst, b):
            if b < NU:
                for n in range(NH):
                    head_pass(dst, b % 4, b - b % 4 + n, n == 0, n == NH - 1)
            else:
                mx_pass(dst, wd_codes[:], wd_scales[:], b, True, True)

        def new_m(b):
            m = psum.tile([P, D], F32, name="m%d" % b, tag="bank%d" % BANK[b])
            m_of[b] = m

        def multiply(u):
            if u < NU:
                n = u % NH
                first = u - n
                for q in range(4):
                    for k in ((n,) if q < 3 or n > 1 else range(2 * n)):
                        if k == 0:
                            new_m(first + q)
                        head_pass(m_of[first + q][:], q, first + k, k == 0, k == NH - 1)
            else:
                new_m(u)
                product(m_of[u][:], u)

        halves = (slice(0, HALF), slice(HALF, D))
        sums_done = []

        def add_sums(count):
            for i in range(len(sums_done), len(sums_done) + count):
                u, h = divmod(i, 2)
                cols_w = slice(P * (u % NH), P * (u % NH) + P)
                w_codes, w_scales = (
                    (wr_codes[:, cols_w], planes[:, 4, cols_w]) if u < NU else (wd_codes[:], wd_scales[:])
                )
                mx_pass(acc[:], w_codes, w_scales, u, i == 0, i == 2 * NB - 1, halves[h])
                sums_done.append(i)

        def squares(m, i):
            nc.scalar.activation(
                out=junk[:, 0 : m.shape[1]], in_=m, func=ACT.Square, bias=negc[:, 0:1], scale=1.0,
                accum_out=ss[:, i : i + 1],
            )

        m_last = []
        for s in range(NB + 1):
            if s < NB:
                regroup(s, EARLY.get(s, SHARE[len(SQ.get(s, ()))]))
            if s == 0:
                words = wr_grp[:].bitcast(F32).rearrange("p (n o e) -> p n o e", n=NH, e=2)
                for i in range(2):
                    nc.scalar.copy(out=words[:, 2 * i : 2 * i + 2], in_=wps[i][:].rearrange("p n e o -> p n o e"))
                quantise(0)
                nc.vector.quantize_mx(out=wr_codes[:].bitcast(FP8X4), scales=planes[:, 4, :], in_=wr_grp[:])
                for q in range(4):
                    rows = slice(32 * q, 32 * q + 32)
                    nc.vector.tensor_copy(
                        out=planes[rows, q, :].bitcast(I32), in_=planes[rows, 4, :].bitcast(I32)
                    )
            if s == 1:
                nc.scalar.copy(
                    out=wd_grp[:].bitcast(F32).rearrange("p (o e) -> p o e", e=2),
                    in_=wpd[:].rearrange("p e o -> p o e"),
                )
            if 2 <= s < NB:
                quantise(s - 1)
            if s == 3:
                nc.vector.quantize_mx(out=wd_codes[:].bitcast(FP8X4), scales=wd_scales[:], in_=wd_grp[:])
            if 1 <= s < NB:
                multiply(s - 1)
            add_sums(SUMS.get(s, 0))
            if s == NB:
                for h in range(2):
                    quantise(NB - 1, halves[h])
                    m = psum.tile([P, HALF], F32, name="m%d_%d" % (NB - 1, h), tag="bank%d" % BANK_LAST[h])
                    m_last.append(m)
                    mx_pass(m[:], wd_codes[:], wd_scales[:], NB - 1, True, True, halves[h])
                    add_sums(1)
            if s == 6:
                nc.scalar.activation(
                    out=junk[:, 0:PIV], in_=m_of[0][:, 0:PIV], func=ACT.Identity, scale=-1.0 / PIV, accum_out=negc[:]
                )
            for b in SQ.get(s, ()):
                squares(m_of[b][:], b)
        inv = 1.0 / (NB * D)
        ssp = small.tile([P, 1], F32, name="ssp")
        part = []
        for i in range(3):
            p_ = small.tile([P, 1], F32, name="part%d" % i)
            part.append(p_)
        s1 = small.tile([P, 1], F32, name="s1")
        delta = small.tile([P, 1], F32, name="delta")
        negv = small.tile([P, 1], F32, name="negv")
        nmean = small.tile([P, 1], F32, name="nmean")
        ngm = small.tile([P, 1], F32, name="ngm")
        rstd = small.tile([P, 1], F32, name="rstd")
        gain = small.tile([P, 1], F32, name="gain")
        gain_v = small.tile([P, 1], F32, name="gain_v")
        shift = small.tile([P, 1], F32, name="shift")
        nc.vector.reduce_sum(out=ssp[:], in_=ss[:, 0 : NB - 2], axis=AX.X)
        nc.vector.tensor_scalar(out=part[0][:], in0=ssp[:], scalar1=inv, scalar2=EPS, op0=ALU.mult, op1=ALU.add)
        for h in range(2):
            squares(m_last[h][:], NB - 1 + h)
        for i in range(2):
            nc.vector.scalar_tensor_tensor(
                out=part[i + 1][:], in0=ss[:, NB - 2 + i : NB - 1 + i], scalar=inv, in1=part[i][:],
                op0=ALU.mult, op1=ALU.add,
            )
        nc.vector.reduce_sum(out=s1[:], in_=acc[:], axis=AX.X)
        nc.vector.tensor_scalar(out=delta[:], in0=s1[:], scalar1=inv, scalar2=negc[:, 0:1], op0=ALU.mult, op1=ALU.add)
        nc.vector.scalar_tensor_tensor(
            out=negv[:], in0=delta[:], scalar=delta[:, 0:1], in1=part[2][:], op0=ALU.mult, op1=ALU.subtract
        )
        nc.vector.tensor_copy(out=g32[:], in_=g_bf[:])
        nc.vector.tensor_copy(out=b32[:], in_=b_bf[:])
        nc.vector.tensor_scalar(out=nmean[:], in0=s1[:], scalar1=-inv, scalar2=None, op0=ALU.mult)
        nc.vector.tensor_tensor(out=ngm[:], in0=nmean[:], in1=g32[:], op=ALU.mult)
        nc.scalar.activation(
            out=rstd[:], in_=ss[:, NB : NB + 1], func=ACT.Abs_reciprocal_sqrt, bias=negv[:, 0:1], scale=-inv
        )
        nc.scalar.activation(out=gain[:], in_=rstd[:], func=ACT.Copy, scale=g32[:, 0:1])
        nc.vector.scalar_tensor_tensor(
            out=shift[:], in0=ngm[:], scalar=rstd[:, 0:1], in1=b32[:], op0=ALU.mult, op1=ALU.add
        )
        nc.vector.tensor_tensor(out=gain_v[:], in0=g32[:], in1=rstd[:], op=ALU.mult)

        freed = (7,) + BANK_LAST + tuple(BANK[b] for b in KEPT) + (7,) + BANK_LAST

        def remake(i):
            b = AGAIN[i]
            m = psum.tile([P, D], F32, name="r%d" % b, tag="bank%d" % freed[i])
            m_of[b] = m
            product(m[:], b)

        def on_scalar(dst, m):
            nc.scalar.activation(out=dst, in_=m, func=ACT.Relu, bias=shift[:, 0:1], scale=gain[:, 0:1])

        def on_vector(dst, m):
            nc.vector.tensor_scalar(
                out=dst, in0=m, scalar1=gain_v[:, 0:1], scalar2=shift[:, 0:1], op0=ALU.mult, op1=ALU.add
            )
            nc.vector.tensor_scalar_max(out=dst, in0=dst, scalar1=0.0)

        remake(0)
        o = outp.tile([P, D], F32, name="o%d" % (NB - 1))
        on_scalar(o[:, halves[0]], m_last[0][:])
        on_vector(o[:, halves[1]], m_last[1][:])
        for h in range(2):
            nc.sync.dma_start(out=out[NB - 1, :, halves[h]], in_=o[:, halves[h]])
        remake(1)
        remake(2)
        for i, b in enumerate(KEPT + AGAIN):
            o = outp.tile([P, D], F32, name="o%d" % b)
            if i % 3 != 1:
                on_scalar(o[:], m_of[b][:])
            else:
                on_vector(o[:], m_of[b][:])
            nc.sync.dma_start(out=out[b], in_=o[:])
            if i + 3 < len(AGAIN):
                remake(i + 3)
